import numpy as np
import ml_dtypes

BF16 = ml_dtypes.bfloat16


def bf(x):
    return np.asarray(x, np.float32).astype(BF16)


def f32(x):
    return np.asarray(x, np.float32)


def f64(x):
    return np.asarray(x).astype(np.float64)


def striped(idx):
    return np.tile(idx.reshape(-1, 16).T, (8, 1))


C, F, S, N = 512, 1024, 512, 128
EPS = 1e-5


def ln(v, gain, shift):
    m = v.mean(axis=0, keepdims=True)
    s = ((v - m) ** 2).mean(axis=0, keepdims=True)
    return gain * (v - m) / np.sqrt(s + EPS) + shift


def setup_inputs():
    base = f32(np.random.standard_normal((C, S)))
    x = f32(np.random.standard_normal((C, N)) * (0.5 + np.random.rand(1, N)) + 0.5 * np.random.standard_normal((1, N)))
    gain_a = f32(0.7 + 0.1 * np.random.standard_normal((C, 1)))
    shift_a = f32(0.3 + 0.1 * np.random.standard_normal((C, 1)))
    gain_b = f32(1.0 + 0.1 * np.random.standard_normal((C, 1)))
    shift_b = f32(0.1 * np.random.standard_normal((C, 1)))
    w1 = bf(np.random.standard_normal((C, F)) / np.sqrt(C))
    b1 = f32(0.1 * np.random.standard_normal((F, 1)))
    w2 = bf(np.random.standard_normal((F, C)) * np.sqrt(2.0 / F))
    b2 = f32(0.1 * np.random.standard_normal((C, 1)))
    return {"base": base, "x": x, "gain_a": gain_a, "shift_a": shift_a, "gain_b": gain_b, "shift_b": shift_b, "w1": w1, "b1": b1, "w2": w2, "b2": b2, "offs": striped(np.random.permutation(S)[:N])}


def reference(base, x, gain_a, shift_a, gain_b, shift_b, w1, b1, w2, b2, offs):
    idx = offs[:16].T.reshape(-1)
    t = ln(f64(x), f64(gain_a), f64(shift_a))
    y = ln(t, f64(gain_b), f64(shift_b))
    h = np.maximum(f64(w1).T @ y + f64(b1), 0.0)
    u = f64(w2).T @ h + f64(b2)
    out = f64(base).copy()
    out[:, idx] = t + u
    return out

@@ -1,0 +1,136 @@
+import concourse.mybir as mybir
+from concourse.masks import make_identity
+
+F32 = mybir.dt.float32
+BF16 = mybir.dt.bfloat16
+U16 = mybir.dt.uint16
+ALU = mybir.AluOpType
+ACT = mybir.ActivationFunctionType
+
+P = 128
+C, F, S, N = 512, 1024, 512, 128
+CB = C // P
+FB = F // P
+EPS = 1e-5
+FLOPS = 2 * 2 * C * F * N
+
+ROW_GAIN_B, ROW_SHIFT_B, ROW_B2, ROW_B1 = 0, CB, 2 * CB, 3 * CB
+N_ROWS = 3 * CB + FB
+
+
+def block(i):
+    return slice(i * P, (i + 1) * P)
+
+
+def tile_crossdecoderlayer_kernel(
+    tc, base, x, gain_a, shift_a, gain_b, shift_b, w1, b1, w2, b2, offs, out
+):
+    nc = tc.nc
+    with (
+        tc.tile_pool(name="held", bufs=1) as held,
+        tc.tile_pool(name="ring", bufs=2) as ring,
+        tc.psum_pool(name="flipped", bufs=1) as flipped,
+        tc.psum_pool(name="products", bufs=2) as products,
+    ):
+        offsets = held.tile([P, N // 16], U16, name="offsets")
+        nc.sync.dma_start(offsets[:], offs)
+        x_cm = held.tile([P, CB, N], F32, name="x_cm")
+        nc.sync.dma_start(x_cm[:], x.rearrange("(b p) j -> p b j", p=P))
+        gain_a_rows = held.tile([P, C], F32, name="gain_a_rows")
+        nc.sync.dma_start(gain_a_rows[:], gain_a.rearrange("c o -> (c o)").partition_broadcast(P))
+        shift_a_rows = held.tile([P, C], F32, name="shift_a_rows")
+        nc.sync.dma_start(shift_a_rows[:], shift_a.rearrange("c o -> (c o)").partition_broadcast(P))
+        w1_sb = held.tile([P, CB, F], BF16, name="w1_sb")
+        nc.sync.dma_start(w1_sb[:], w1.rearrange("(b p) k -> p b k", p=P))
+        w2_sb = held.tile([P, FB, C], BF16, name="w2_sb")
+        nc.sync.dma_start(w2_sb[:], w2.rearrange("(kb p) c -> p kb c", p=P))
+        windows = [held.tile([P, S], F32, name=f"window{b}") for b in range(CB)]
+        for b in range(CB):
+            nc.sync.dma_start(windows[b][:], base[block(b), :])
+
+        identity = held.tile([P, P], F32, name="identity")
+        make_identity(nc, identity[:])
+        eps_col = held.tile([P, 1], F32, name="eps_col")
+        nc.gpsimd.memset(eps_col[:], EPS)
+
+        vec_rows = held.tile([P, P], F32, name="vec_rows")
+        nc.gpsimd.memset(vec_rows[:], 0.0)
+        for row, vec in ((ROW_GAIN_B, gain_b), (ROW_SHIFT_B, shift_b), (ROW_B2, b2), (ROW_B1, b1)):
+            as_rows = vec.rearrange("(r p) o -> r (p o)", p=P)
+            nc.scalar.dma_start(vec_rows[row : row + as_rows.shape[0], :], as_rows)
+        vec_ps = flipped.tile([P, P], F32, name="vec_ps")
+        nc.tensor.transpose(vec_ps[:], vec_rows[:], identity[:])
+        vec_cols = held.tile([P, N_ROWS], F32, name="vec_cols")
+        nc.vector.tensor_copy(vec_cols[:], vec_ps[:, 0:N_ROWS])
+
+        x_tm = flipped.tile([P, C], F32, name="x_tm")
+        for b in range(CB):
+            nc.tensor.transpose(x_tm[:, block(b)], x_cm[:, b, :], identity[:])
+
+        stats_x = held.tile([P, 6], F32, name="stats_x")
+        nc.vector.bn_stats(stats_x[:], x_tm[:])
+        mean_var_x = held.tile([P, 2], F32, name="mean_var_x")
+        nc.vector.bn_aggr(mean_var_x[:], stats_x[:])
+        std_x = held.tile([P, 1], F32, name="std_x")
+        nc.scalar.activation(std_x[:], mean_var_x[:, 1:2], ACT.Sqrt, bias=eps_col[:])
+        centred_gained = held.tile([P, C], F32, name="centred_gained")
+        nc.vector.scalar_tensor_tensor(
+            centred_gained[:], x_tm[:], mean_var_x[:, 0:1], gain_a_rows[:], ALU.subtract, ALU.mult
+        )
+        rstd_x = held.tile([P, 1], F32, name="rstd_x")
+        nc.vector.reciprocal(rstd_x[:], std_x[:])
+        t_tm = held.tile([P, C], F32, name="t_tm")
+        nc.vector.scalar_tensor_tensor(
+            t_tm[:], centred_gained[:], rstd_x[:], shift_a_rows[:], ALU.mult, ALU.add
+        )
+
+        t_ps = flipped.tile([P, CB * N], F32, name="t_ps")
+        for b in range(CB):
+            nc.tensor.transpose(t_ps[:, block(b)], t_tm[:, block(b)], identity[:])
+
+        stats_t = held.tile([P, 6], F32, name="stats_t")
+        nc.vector.bn_stats(stats_t[:], t_tm[:])
+        mean_var_t = held.tile([P, 2], F32, name="mean_var_t")
+        nc.vector.bn_aggr(mean_var_t[:], stats_t[:])
+        std_t = held.tile([P, 1], F32, name="std_t")
+        nc.scalar.activation(std_t[:], mean_var_t[:, 1:2], ACT.Sqrt, bias=eps_col[:])
+        rstd_t = held.tile([P, 1], F32, name="rstd_t")
+        nc.vector.reciprocal(rstd_t[:], std_t[:])
+        normed_tm = held.tile([P, C], F32, name="normed_tm")
+        nc.vector.tensor_scalar(
+            normed_tm[:], t_tm[:], mean_var_t[:, 0:1], rstd_t[:], ALU.subtract, ALU.mult
+        )
+        normed_ps = flipped.tile([P, CB * N], F32, name="normed_ps")
+        for b in range(CB):
+            nc.tensor.transpose(normed_ps[:, block(b)], normed_tm[:, block(b)], identity[:])
+
+        y = held.tile([P, CB, N], BF16, name="y")
+        for b in range(CB):
+            gain_col = vec_cols[:, ROW_GAIN_B + b : ROW_GAIN_B + b + 1]
+            shift_col = vec_cols[:, ROW_SHIFT_B + b : ROW_SHIFT_B + b + 1]
+            if b % 2 == 0:
+                nc.scalar.activation(y[:, b, :], normed_ps[:, block(b)], ACT.Identity, bias=shift_col, scale=gain_col)
+            else:
+                nc.vector.tensor_scalar(y[:, b, :], normed_ps[:, block(b)], gain_col, shift_col, ALU.mult, ALU.add)
+        t_cm = held.tile([P, CB * N], F32, name="t_cm")
+        nc.vector.tensor_copy(t_cm[:], t_ps[:])
+
+        h = held.tile([P, FB, N], BF16, name="h")
+        for kb in range(FB):
+            h_ps = products.tile([P, N], F32, name="h_ps")
+            for b in range(CB):
+                nc.tensor.matmul(h_ps[:], w1_sb[:, b, block(kb)], y[:, b, :], start=(b == 0), stop=(b == CB - 1))
+            b1_col = vec_cols[:, ROW_B1 + kb : ROW_B1 + kb + 1]
+            if kb % 2 == 0:
+                nc.scalar.activation(h[:, kb, :], h_ps[:], ACT.Relu, bias=b1_col)
+            else:
+                nc.vector.tensor_scalar(h[:, kb, :], h_ps[:], b1_col, 0.0, ALU.add, ALU.max)
+
+        for b in range(CB):
+            u_ps = products.tile([P, N], F32, name="u_ps")
+            for kb in range(FB):
+                nc.tensor.matmul(u_ps[:], w2_sb[:, kb, block(b)], h[:, kb, :], start=(kb == 0), stop=(kb == FB - 1))
+            u = ring.tile([P, N], F32, name="u")
+            nc.scalar.activation(u[:], u_ps[:], ACT.Identity, bias=vec_cols[:, ROW_B2 + b : ROW_B2 + b + 1])
+            nc.vector.tensor_tensor(windows[b][:].indirect(offsets[:]), t_cm[:, block(b)], u[:], ALU.add)
+            nc.sync.dma_start(out[block(b), :], windows[b][:])

@@ -11,7 +11,12 @@ P = 128
 C, F, S, N = 512, 1024, 512, 128
 CB = C // P
 FB = F // P
+HALVES = 2
+HB = CB // HALVES
+HC = C // HALVES
 EPS = 1e-5
+BN_STATS_DIM = 6
+PSUM_BANKS = 8
 FLOPS = 2 * 2 * C * F * N
 
 ROW_GAIN_B, ROW_SHIFT_B, ROW_B2, ROW_B1 = 0, CB, 2 * CB, 3 * CB
@@ -22,6 +27,10 @@ def block(i):
     return slice(i * P, (i + 1) * P)
 
 
+def half(i):
+    return slice(i * HC, (i + 1) * HC)
+
+
 def tile_crossdecoderlayer_kernel(
     tc, base, x, gain_a, shift_a, gain_b, shift_b, w1, b1, w2, b2, offs, out
 ):
@@ -29,17 +38,34 @@ def tile_crossdecoderlayer_kernel(
     with (
         tc.tile_pool(name="held", bufs=1) as held,
         tc.tile_pool(name="ring", bufs=2) as ring,
-        tc.psum_pool(name="flipped", bufs=1) as flipped,
-        tc.psum_pool(name="products", bufs=2) as products,
+        tc.psum_pool(name="psum", bufs=PSUM_BANKS) as psum,
     ):
-        offsets = held.tile([P, N // 16], U16, name="offsets")
-        nc.sync.dma_start(offsets[:], offs)
+
+        def psum_bank(width, name):
+            return psum.tile([P, width], F32, name=name, tag="bank")
+
+        def mean_and_rstd(halves, name):
+            stats = held.tile([P, HALVES * BN_STATS_DIM], F32, name=f"stats_{name}")
+            for i in range(HALVES):
+                nc.vector.bn_stats(stats[:, i * BN_STATS_DIM : (i + 1) * BN_STATS_DIM], halves[i])
+            mean_var = held.tile([P, 2], F32, name=f"mean_var_{name}")
+            nc.vector.bn_aggr(mean_var[:], stats[:])
+            std = held.tile([P, 1], F32, name=f"std_{name}")
+            nc.scalar.activation(std[:], mean_var[:, 1:2], ACT.Sqrt, bias=eps_col[:])
+            rstd = held.tile([P, 1], F32, name=f"rstd_{name}")
+            nc.vector.reciprocal(rstd[:], std[:])
+            return mean_var[:, 0:1], rstd[:]
+
         x_cm = held.tile([P, CB, N], F32, name="x_cm")
-        nc.sync.dma_start(x_cm[:], x.rearrange("(b p) j -> p b j", p=P))
+        x_blocks = x.rearrange("(b p) j -> p b j", p=P)
+        for i in range(HALVES):
+            nc.sync.dma_start(x_cm[:, i * HB : (i + 1) * HB, :], x_blocks[:, i * HB : (i + 1) * HB, :])
         gain_a_rows = held.tile([P, C], F32, name="gain_a_rows")
         nc.sync.dma_start(gain_a_rows[:], gain_a.rearrange("c o -> (c o)").partition_broadcast(P))
         shift_a_rows = held.tile([P, C], F32, name="shift_a_rows")
         nc.sync.dma_start(shift_a_rows[:], shift_a.rearrange("c o -> (c o)").partition_broadcast(P))
+        offsets = held.tile([P, N // 16], U16, name="offsets")
+        nc.sync.dma_start(offsets[:], offs)
         w1_sb = held.tile([P, CB, F], BF16, name="w1_sb")
         nc.sync.dma_start(w1_sb[:], w1.rearrange("(b p) k -> p b k", p=P))
         w2_sb = held.tile([P, FB, C], BF16, name="w2_sb")
@@ -54,70 +80,58 @@ def tile_crossdecoderlayer_kernel(
         nc.gpsimd.memset(eps_col[:], EPS)
 
         vec_rows = held.tile([P, P], F32, name="vec_rows")
-        nc.gpsimd.memset(vec_rows[:], 0.0)
+        nc.vector.memset(vec_rows[:], 0.0)
         for row, vec in ((ROW_GAIN_B, gain_b), (ROW_SHIFT_B, shift_b), (ROW_B2, b2), (ROW_B1, b1)):
             as_rows = vec.rearrange("(r p) o -> r (p o)", p=P)
             nc.scalar.dma_start(vec_rows[row : row + as_rows.shape[0], :], as_rows)
-        vec_ps = flipped.tile([P, P], F32, name="vec_ps")
-        nc.tensor.transpose(vec_ps[:], vec_rows[:], identity[:])
-        vec_cols = held.tile([P, N_ROWS], F32, name="vec_cols")
-        nc.vector.tensor_copy(vec_cols[:], vec_ps[:, 0:N_ROWS])
 
-        x_tm = flipped.tile([P, C], F32, name="x_tm")
+        x_tm = [psum_bank(HC, f"x_tm{i}") for i in range(HALVES)]
         for b in range(CB):
-            nc.tensor.transpose(x_tm[:, block(b)], x_cm[:, b, :], identity[:])
+            nc.tensor.transpose(x_tm[b // HB][:, block(b % HB)], x_cm[:, b, :], identity[:])
+        vec_ps = psum_bank(P, "vec_ps")
+        nc.tensor.transpose(vec_ps[:], vec_rows[:], identity[:])
 
-        stats_x = held.tile([P, 6], F32, name="stats_x")
-        nc.vector.bn_stats(stats_x[:], x_tm[:])
-        mean_var_x = held.tile([P, 2], F32, name="mean_var_x")
-        nc.vector.bn_aggr(mean_var_x[:], stats_x[:])
-        std_x = held.tile([P, 1], F32, name="std_x")
-        nc.scalar.activation(std_x[:], mean_var_x[:, 1:2], ACT.Sqrt, bias=eps_col[:])
+        mean_x, rstd_x = mean_and_rstd([x_tm[i][:] for i in range(HALVES)], "x")
         centred_gained = held.tile([P, C], F32, name="centred_gained")
-        nc.vector.scalar_tensor_tensor(
-            centred_gained[:], x_tm[:], mean_var_x[:, 0:1], gain_a_rows[:], ALU.subtract, ALU.mult
-        )
-        rstd_x = held.tile([P, 1], F32, name="rstd_x")
-        nc.vector.reciprocal(rstd_x[:], std_x[:])
+        for i in range(HALVES):
+            nc.vector.scalar_tensor_tensor(
+                centred_gained[:, half(i)], x_tm[i][:], mean_x, gain_a_rows[:, half(i)], ALU.subtract, ALU.mult
+            )
         t_tm = held.tile([P, C], F32, name="t_tm")
-        nc.vector.scalar_tensor_tensor(
-            t_tm[:], centred_gained[:], rstd_x[:], shift_a_rows[:], ALU.mult, ALU.add
-        )
+        for i in range(HALVES):
+            nc.vector.scalar_tensor_tensor(
+                t_tm[:, half(i)], centred_gained[:, half(i)], rstd_x, shift_a_rows[:, half(i)], ALU.mult, ALU.add
+            )
 
-        t_ps = flipped.tile([P, CB * N], F32, name="t_ps")
+        t_ps = psum_bank(C, "t_ps")
         for b in range(CB):
             nc.tensor.transpose(t_ps[:, block(b)], t_tm[:, block(b)], identity[:])
 
-        stats_t = held.tile([P, 6], F32, name="stats_t")
-        nc.vector.bn_stats(stats_t[:], t_tm[:])
-        mean_var_t = held.tile([P, 2], F32, name="mean_var_t")
-        nc.vector.bn_aggr(mean_var_t[:], stats_t[:])
-        std_t = held.tile([P, 1], F32, name="std_t")
-        nc.scalar.activation(std_t[:], mean_var_t[:, 1:2], ACT.Sqrt, bias=eps_col[:])
-        rstd_t = held.tile([P, 1], F32, name="rstd_t")
-        nc.vector.reciprocal(rstd_t[:], std_t[:])
+        mean_t, rstd_t = mean_and_rstd([t_tm[:, half(i)] for i in range(HALVES)], "t")
         normed_tm = held.tile([P, C], F32, name="normed_tm")
-        nc.vector.tensor_scalar(
-            normed_tm[:], t_tm[:], mean_var_t[:, 0:1], rstd_t[:], ALU.subtract, ALU.mult
-        )
-        normed_ps = flipped.tile([P, CB * N], F32, name="normed_ps")
+        for i in range(HALVES):
+            nc.vector.tensor_scalar(normed_tm[:, half(i)], t_tm[:, half(i)], mean_t, rstd_t, ALU.subtract, ALU.mult)
+        normed_ps = [psum_bank(HC, f"normed_ps{i}") for i in range(HALVES)]
         for b in range(CB):
-            nc.tensor.transpose(normed_ps[:, block(b)], normed_tm[:, block(b)], identity[:])
+            nc.tensor.transpose(normed_ps[b // HB][:, block(b % HB)], normed_tm[:, block(b)], identity[:])
 
+        vec_cols = held.tile([P, N_ROWS], F32, name="vec_cols")
+        nc.vector.tensor_copy(vec_cols[:], vec_ps[:, 0:N_ROWS])
         y = held.tile([P, CB, N], BF16, name="y")
         for b in range(CB):
+            normed_block = normed_ps[b // HB][:, block(b % HB)]
             gain_col = vec_cols[:, ROW_GAIN_B + b : ROW_GAIN_B + b + 1]
             shift_col = vec_cols[:, ROW_SHIFT_B + b : ROW_SHIFT_B + b + 1]
-            if b % 2 == 0:
-                nc.scalar.activation(y[:, b, :], normed_ps[:, block(b)], ACT.Identity, bias=shift_col, scale=gain_col)
+            if b // HB == 0:
+                nc.scalar.activation(y[:, b, :], normed_block, ACT.Identity, bias=shift_col, scale=gain_col)
             else:
-                nc.vector.tensor_scalar(y[:, b, :], normed_ps[:, block(b)], gain_col, shift_col, ALU.mult, ALU.add)
-        t_cm = held.tile([P, CB * N], F32, name="t_cm")
+                nc.vector.tensor_scalar(y[:, b, :], normed_block, gain_col, shift_col, ALU.mult, ALU.add)
+        t_cm = held.tile([P, C], F32, name="t_cm")
         nc.vector.tensor_copy(t_cm[:], t_ps[:])
 
         h = held.tile([P, FB, N], BF16, name="h")
         for kb in range(FB):
-            h_ps = products.tile([P, N], F32, name="h_ps")
+            h_ps = psum_bank(N, "h_ps")
             for b in range(CB):
                 nc.tensor.matmul(h_ps[:], w1_sb[:, b, block(kb)], y[:, b, :], start=(b == 0), stop=(b == CB - 1))
             b1_col = vec_cols[:, ROW_B1 + kb : ROW_B1 + kb + 1]
@@ -127,7 +141,7 @@ def tile_crossdecoderlayer_kernel(
                 nc.vector.tensor_scalar(h[:, kb, :], h_ps[:], b1_col, 0.0, ALU.add, ALU.max)
 
         for b in range(CB):
-            u_ps = products.tile([P, N], F32, name="u_ps")
+            u_ps = psum_bank(N, "u_ps")
             for kb in range(FB):
                 nc.tensor.matmul(u_ps[:], w2_sb[:, kb, block(b)], h[:, kb, :], start=(kb == 0), stop=(kb == FB - 1))
             u = ring.tile([P, N], F32, name="u")

@@ -50,10 +50,8 @@ def tile_crossdecoderlayer_kernel(
                 nc.vector.bn_stats(stats[:, i * BN_STATS_DIM : (i + 1) * BN_STATS_DIM], halves[i])
             mean_var = held.tile([P, 2], F32, name=f"mean_var_{name}")
             nc.vector.bn_aggr(mean_var[:], stats[:])
-            std = held.tile([P, 1], F32, name=f"std_{name}")
-            nc.scalar.activation(std[:], mean_var[:, 1:2], ACT.Sqrt, bias=eps_col[:])
             rstd = held.tile([P, 1], F32, name=f"rstd_{name}")
-            nc.vector.reciprocal(rstd[:], std[:])
+            nc.scalar.activation(rstd[:], mean_var[:, 1:2], ACT.Abs_reciprocal_sqrt, bias=eps_col[:])
             return mean_var[:, 0:1], rstd[:]
 
         x_cm = held.tile([P, CB, N], F32, name="x_cm")

@@ -11,9 +11,6 @@ P = 128
 C, F, S, N = 512, 1024, 512, 128
 CB = C // P
 FB = F // P
-HALVES = 2
-HB = CB // HALVES
-HC = C // HALVES
 EPS = 1e-5
 BN_STATS_DIM = 6
 PSUM_BANKS = 8
@@ -25,10 +22,6 @@ N_ROWS = 3 * CB + FB
 
 def block(i):
     return slice(i * P, (i + 1) * P)
-
-
-def half(i):
-    return slice(i * HC, (i + 1) * HC)
 
 
 def tile_crossdecoderlayer_kernel(
@@ -44,10 +37,10 @@ def tile_crossdecoderlayer_kernel(
         def psum_bank(width, name):
             return psum.tile([P, width], F32, name=name, tag="bank")
 
-        def mean_and_rstd(halves, name):
-            stats = held.tile([P, HALVES * BN_STATS_DIM], F32, name=f"stats_{name}")
-            for i in range(HALVES):
-                nc.vector.bn_stats(stats[:, i * BN_STATS_DIM : (i + 1) * BN_STATS_DIM], halves[i])
+        def mean_and_rstd(blocks, name):
+            stats = held.tile([P, CB * BN_STATS_DIM], F32, name=f"stats_{name}")
+            for b in range(CB):
+                nc.vector.bn_stats(stats[:, b * BN_STATS_DIM : (b + 1) * BN_STATS_DIM], blocks[b])
             mean_var = held.tile([P, 2], F32, name=f"mean_var_{name}")
             nc.vector.bn_aggr(mean_var[:], stats[:])
             rstd = held.tile([P, 1], F32, name=f"rstd_{name}")
@@ -56,8 +49,8 @@ def tile_crossdecoderlayer_kernel(
 
         x_cm = held.tile([P, CB, N], F32, name="x_cm")
         x_blocks = x.rearrange("(b p) j -> p b j", p=P)
-        for i in range(HALVES):
-            nc.sync.dma_start(x_cm[:, i * HB : (i + 1) * HB, :], x_blocks[:, i * HB : (i + 1) * HB, :])
+        for b in range(CB):
+            nc.sync.dma_start(x_cm[:, b, :], x_blocks[:, b, :])
         gain_a_rows = held.tile([P, C], F32, name="gain_a_rows")
         nc.sync.dma_start(gain_a_rows[:], gain_a.rearrange("c o -> (c o)").partition_broadcast(P))
         shift_a_rows = held.tile([P, C], F32, name="shift_a_rows")
@@ -83,47 +76,46 @@ def tile_crossdecoderlayer_kernel(
             as_rows = vec.rearrange("(r p) o -> r (p o)", p=P)
             nc.scalar.dma_start(vec_rows[row : row + as_rows.shape[0], :], as_rows)
 
-        x_tm = [psum_bank(HC, f"x_tm{i}") for i in range(HALVES)]
+        x_tm = [psum_bank(P, f"x_tm{b}") for b in range(CB)]
         for b in range(CB):
-            nc.tensor.transpose(x_tm[b // HB][:, block(b % HB)], x_cm[:, b, :], identity[:])
+            nc.tensor.transpose(x_tm[b][:], x_cm[:, b, :], identity[:])
         vec_ps = psum_bank(P, "vec_ps")
         nc.tensor.transpose(vec_ps[:], vec_rows[:], identity[:])
 
-        mean_x, rstd_x = mean_and_rstd([x_tm[i][:] for i in range(HALVES)], "x")
+        mean_x, rstd_x = mean_and_rstd([x_tm[b][:] for b in range(CB)], "x")
         centred_gained = held.tile([P, C], F32, name="centred_gained")
-        for i in range(HALVES):
+        for b in range(CB):
             nc.vector.scalar_tensor_tensor(
-                centred_gained[:, half(i)], x_tm[i][:], mean_x, gain_a_rows[:, half(i)], ALU.subtract, ALU.mult
+                centred_gained[:, block(b)], x_tm[b][:], mean_x, gain_a_rows[:, block(b)], ALU.subtract, ALU.mult
             )
         t_tm = held.tile([P, C], F32, name="t_tm")
-        for i in range(HALVES):
+        for b in range(CB):
             nc.vector.scalar_tensor_tensor(
-                t_tm[:, half(i)], centred_gained[:, half(i)], rstd_x, shift_a_rows[:, half(i)], ALU.mult, ALU.add
+                t_tm[:, block(b)], centred_gained[:, block(b)], rstd_x, shift_a_rows[:, block(b)], ALU.mult, ALU.add
             )
 
         t_ps = psum_bank(C, "t_ps")
         for b in range(CB):
             nc.tensor.transpose(t_ps[:, block(b)], t_tm[:, block(b)], identity[:])
 
-        mean_t, rstd_t = mean_and_rstd([t_tm[:, half(i)] for i in range(HALVES)], "t")
+        mean_t, rstd_t = mean_and_rstd([t_tm[:, block(b)] for b in range(CB)], "t")
         normed_tm = held.tile([P, C], F32, name="normed_tm")
-        for i in range(HALVES):
-            nc.vector.tensor_scalar(normed_tm[:, half(i)], t_tm[:, half(i)], mean_t, rstd_t, ALU.subtract, ALU.mult)
-        normed_ps = [psum_bank(HC, f"normed_ps{i}") for i in range(HALVES)]
         for b in range(CB):
-            nc.tensor.transpose(normed_ps[b // HB][:, block(b % HB)], normed_tm[:, block(b)], identity[:])
+            nc.vector.tensor_scalar(normed_tm[:, block(b)], t_tm[:, block(b)], mean_t, rstd_t, ALU.subtract, ALU.mult)
+        normed_ps = [psum_bank(P, f"normed_ps{b}") for b in range(CB)]
+        for b in range(CB):
+            nc.tensor.transpose(normed_ps[b][:], normed_tm[:, block(b)], identity[:])
 
         vec_cols = held.tile([P, N_ROWS], F32, name="vec_cols")
         nc.vector.tensor_copy(vec_cols[:], vec_ps[:, 0:N_ROWS])
         y = held.tile([P, CB, N], BF16, name="y")
         for b in range(CB):
-            normed_block = normed_ps[b // HB][:, block(b % HB)]
             gain_col = vec_cols[:, ROW_GAIN_B + b : ROW_GAIN_B + b + 1]
             shift_col = vec_cols[:, ROW_SHIFT_B + b : ROW_SHIFT_B + b + 1]
-            if b // HB == 0:
-                nc.scalar.activation(y[:, b, :], normed_block, ACT.Identity, bias=shift_col, scale=gain_col)
+            if b % 2 == 0:
+                nc.scalar.activation(y[:, b, :], normed_ps[b][:], ACT.Identity, bias=shift_col, scale=gain_col)
             else:
-                nc.vector.tensor_scalar(y[:, b, :], normed_block, gain_col, shift_col, ALU.mult, ALU.add)
+                nc.vector.tensor_scalar(y[:, b, :], normed_ps[b][:], gain_col, shift_col, ALU.mult, ALU.add)
         t_cm = held.tile([P, C], F32, name="t_cm")
         nc.vector.tensor_copy(t_cm[:], t_ps[:])
 

@@ -19,6 +19,8 @@ FLOPS = 2 * 2 * C * F * N
 ROW_GAIN_B, ROW_SHIFT_B, ROW_B2, ROW_B1 = 0, CB, 2 * CB, 3 * CB
 N_ROWS = 3 * CB + FB
 
+WARM_AFTER_X, WARM_AFTER_T, WARM_AFTER_NORMED = 3, 2, 1
+
 
 def block(i):
     return slice(i * P, (i + 1) * P)
@@ -46,6 +48,10 @@ def tile_crossdecoderlayer_kernel(
             rstd = held.tile([P, 1], F32, name=f"rstd_{name}")
             nc.scalar.activation(rstd[:], mean_var[:, 1:2], ACT.Abs_reciprocal_sqrt, bias=eps_col[:])
             return mean_var[:, 0:1], rstd[:]
+
+        def keep_clock_up(n_matmuls, moving):
+            for i in range(n_matmuls):
+                nc.tensor.matmul(unread[:], identity[:], moving, start=True, stop=True)
 
         x_cm = held.tile([P, CB, N], F32, name="x_cm")
         x_blocks = x.rearrange("(b p) j -> p b j", p=P)
@@ -81,6 +87,8 @@ def tile_crossdecoderlayer_kernel(
             nc.tensor.transpose(x_tm[b][:], x_cm[:, b, :], identity[:])
         vec_ps = psum_bank(P, "vec_ps")
         nc.tensor.transpose(vec_ps[:], vec_rows[:], identity[:])
+        unread = psum_bank(P, "unread")
+        keep_clock_up(WARM_AFTER_X, x_cm[:, CB - 1, :])
 
         mean_x, rstd_x = mean_and_rstd([x_tm[b][:] for b in range(CB)], "x")
         centred_gained = held.tile([P, C], F32, name="centred_gained")
@@ -97,6 +105,7 @@ def tile_crossdecoderlayer_kernel(
         t_ps = psum_bank(C, "t_ps")
         for b in range(CB):
             nc.tensor.transpose(t_ps[:, block(b)], t_tm[:, block(b)], identity[:])
+        keep_clock_up(WARM_AFTER_T, t_tm[:, block(CB - 1)])
 
         mean_t, rstd_t = mean_and_rstd([t_tm[:, block(b)] for b in range(CB)], "t")
         normed_tm = held.tile([P, C], F32, name="normed_tm")
@@ -105,6 +114,7 @@ def tile_crossdecoderlayer_kernel(
         normed_ps = [psum_bank(P, f"normed_ps{b}") for b in range(CB)]
         for b in range(CB):
             nc.tensor.transpose(normed_ps[b][:], normed_tm[:, block(b)], identity[:])
+        keep_clock_up(WARM_AFTER_NORMED, normed_tm[:, block(CB - 1)])
 
         vec_cols = held.tile([P, N_ROWS], F32, name="vec_cols")
         nc.vector.tensor_copy(vec_cols[:], vec_ps[:, 0:N_ROWS])

@@ -20,6 +20,8 @@ ROW_GAIN_B, ROW_SHIFT_B, ROW_B2, ROW_B1 = 0, CB, 2 * CB, 3 * CB
 N_ROWS = 3 * CB + FB
 
 WARM_AFTER_X, WARM_AFTER_T, WARM_AFTER_NORMED = 3, 2, 1
+WARM_BEFORE_X = 3
+BANK_F32 = 512
 
 
 def block(i):
@@ -51,7 +53,7 @@ def tile_crossdecoderlayer_kernel(
 
         def keep_clock_up(n_matmuls, moving):
             for i in range(n_matmuls):
-                nc.tensor.matmul(unread[:], identity[:], moving, start=True, stop=True)
+                nc.tensor.matmul(unread[:, 0:P], identity[:], moving, start=True, stop=True)
 
         x_cm = held.tile([P, CB, N], F32, name="x_cm")
         x_blocks = x.rearrange("(b p) j -> p b j", p=P)
@@ -71,6 +73,12 @@ def tile_crossdecoderlayer_kernel(
         for b in range(CB):
             nc.sync.dma_start(windows[b][:], base[block(b), :])
 
+        zeros = held.tile([P, BANK_F32], BF16, name="zeros")
+        nc.vector.memset(zeros[:], 0.0)
+        unread = psum_bank(BANK_F32, "unread")
+        for i in range(WARM_BEFORE_X):
+            nc.tensor.matmul(unread[:], zeros[:, 0:P], zeros[:], start=True, stop=True)
+
         identity = held.tile([P, P], F32, name="identity")
         make_identity(nc, identity[:])
         eps_col = held.tile([P, 1], F32, name="eps_col")
@@ -87,7 +95,6 @@ def tile_crossdecoderlayer_kernel(
             nc.tensor.transpose(x_tm[b][:], x_cm[:, b, :], identity[:])
         vec_ps = psum_bank(P, "vec_ps")
         nc.tensor.transpose(vec_ps[:], vec_rows[:], identity[:])
-        unread = psum_bank(P, "unread")
         keep_clock_up(WARM_AFTER_X, x_cm[:, CB - 1, :])
 
         mean_x, rstd_x = mean_and_rstd([x_tm[b][:] for b in range(CB)], "x")

@@ -19,7 +19,7 @@ FLOPS = 2 * 2 * C * F * N
 ROW_GAIN_B, ROW_SHIFT_B, ROW_B2, ROW_B1 = 0, CB, 2 * CB, 3 * CB
 N_ROWS = 3 * CB + FB
 
-WARM_AFTER_X, WARM_AFTER_T, WARM_AFTER_NORMED = 3, 2, 1
+WARM_AFTER_X, WARM_AFTER_T = 3, 2
 WARM_BEFORE_X = 3
 BANK_F32 = 512
 
@@ -121,7 +121,6 @@ def tile_crossdecoderlayer_kernel(
         normed_ps = [psum_bank(P, f"normed_ps{b}") for b in range(CB)]
         for b in range(CB):
             nc.tensor.transpose(normed_ps[b][:], normed_tm[:, block(b)], identity[:])
-        keep_clock_up(WARM_AFTER_NORMED, normed_tm[:, block(CB - 1)])
 
         vec_cols = held.tile([P, N_ROWS], F32, name="vec_cols")
         nc.vector.tensor_copy(vec_cols[:], vec_ps[:, 0:N_ROWS])

@@ -17,7 +17,7 @@ PSUM_BANKS = 8
 FLOPS = 2 * 2 * C * F * N
 
 ROW_GAIN_B, ROW_SHIFT_B, ROW_B2, ROW_B1 = 0, CB, 2 * CB, 3 * CB
-N_ROWS = 3 * CB + FB
+N_ROWS = 32
 
 WARM_AFTER_X, WARM_AFTER_T = 3, 2
 WARM_BEFORE_X = 3
@@ -63,6 +63,12 @@ def tile_crossdecoderlayer_kernel(
         nc.sync.dma_start(gain_a_rows[:], gain_a.rearrange("c o -> (c o)").partition_broadcast(P))
         shift_a_rows = held.tile([P, C], F32, name="shift_a_rows")
         nc.sync.dma_start(shift_a_rows[:], shift_a.rearrange("c o -> (c o)").partition_broadcast(P))
+
+        vec_rows = held.tile([N_ROWS, P], F32, name="vec_rows")
+        nc.vector.memset(vec_rows[:], 0.0)
+        for row, vec in ((ROW_GAIN_B, gain_b), (ROW_SHIFT_B, shift_b), (ROW_B2, b2), (ROW_B1, b1)):
+            as_rows = vec.rearrange("(r p) o -> r (p o)", p=P)
+            nc.sync.dma_start(vec_rows[row : row + as_rows.shape[0], :], as_rows)
         offsets = held.tile([P, N // 16], U16, name="offsets")
         nc.sync.dma_start(offsets[:], offs)
         w1_sb = held.tile([P, CB, F], BF16, name="w1_sb")
@@ -84,20 +90,16 @@ def tile_crossdecoderlayer_kernel(
         eps_col = held.tile([P, 1], F32, name="eps_col")
         nc.gpsimd.memset(eps_col[:], EPS)
 
-        vec_rows = held.tile([P, P], F32, name="vec_rows")
-        nc.vector.memset(vec_rows[:], 0.0)
-        for row, vec in ((ROW_GAIN_B, gain_b), (ROW_SHIFT_B, shift_b), (ROW_B2, b2), (ROW_B1, b1)):
-            as_rows = vec.rearrange("(r p) o -> r (p o)", p=P)
-            nc.scalar.dma_start(vec_rows[row : row + as_rows.shape[0], :], as_rows)
-
         x_tm = [psum_bank(P, f"x_tm{b}") for b in range(CB)]
         for b in range(CB):
             nc.tensor.transpose(x_tm[b][:], x_cm[:, b, :], identity[:])
-        vec_ps = psum_bank(P, "vec_ps")
-        nc.tensor.transpose(vec_ps[:], vec_rows[:], identity[:])
         keep_clock_up(WARM_AFTER_X, x_cm[:, CB - 1, :])
+        vec_ps = psum_bank(N_ROWS, "vec_ps")
+        nc.tensor.matmul(vec_ps[:], vec_rows[:], identity[0:N_ROWS, 0:N_ROWS], start=True, stop=True)
 
         mean_x, rstd_x = mean_and_rstd([x_tm[b][:] for b in range(CB)], "x")
+        vec_cols = held.tile([P, N_ROWS], F32, name="vec_cols")
+        nc.scalar.activation(vec_cols[:], vec_ps[:], ACT.Copy)
         centred_gained = held.tile([P, C], F32, name="centred_gained")
         for b in range(CB):
             nc.vector.scalar_tensor_tensor(
@@ -122,8 +124,6 @@ def tile_crossdecoderlayer_kernel(
         for b in range(CB):
             nc.tensor.transpose(normed_ps[b][:], normed_tm[:, block(b)], identity[:])
 
-        vec_cols = held.tile([P, N_ROWS], F32, name="vec_cols")
-        nc.vector.tensor_copy(vec_cols[:], vec_ps[:, 0:N_ROWS])
         y = held.tile([P, CB, N], BF16, name="y")
         for b in range(CB):
             gain_col = vec_cols[:, ROW_GAIN_B + b : ROW_GAIN_B + b + 1]

@@ -19,7 +19,9 @@ FLOPS = 2 * 2 * C * F * N
 ROW_GAIN_B, ROW_SHIFT_B, ROW_B2, ROW_B1 = 0, CB, 2 * CB, 3 * CB
 N_ROWS = 32
 
-WARM_AFTER_X, WARM_AFTER_T = 3, 2
+WARM_AFTER_X = 2
+WARM_AFTER_T = 3
+WARM_AFTER_NORMED = 1
 WARM_BEFORE_X = 3
 BANK_F32 = 512
 
@@ -57,8 +59,9 @@ def tile_crossdecoderlayer_kernel(
 
         x_cm = held.tile([P, CB, N], F32, name="x_cm")
         x_blocks = x.rearrange("(b p) j -> p b j", p=P)
-        for b in range(CB):
-            nc.sync.dma_start(x_cm[:, b, :], x_blocks[:, b, :])
+        for half in range(2):
+            blocks = slice(half * CB // 2, (half + 1) * CB // 2)
+            nc.sync.dma_start(x_cm[:, blocks, :], x_blocks[:, blocks, :])
         gain_a_rows = held.tile([P, C], F32, name="gain_a_rows")
         nc.sync.dma_start(gain_a_rows[:], gain_a.rearrange("c o -> (c o)").partition_broadcast(P))
         shift_a_rows = held.tile([P, C], F32, name="shift_a_rows")
@@ -105,15 +108,19 @@ def tile_crossdecoderlayer_kernel(
             nc.vector.scalar_tensor_tensor(
                 centred_gained[:, block(b)], x_tm[b][:], mean_x, gain_a_rows[:, block(b)], ALU.subtract, ALU.mult
             )
+            if b % 2 == 0:
+                keep_clock_up(1, centred_gained[:, block(b)])
         t_tm = held.tile([P, C], F32, name="t_tm")
         for b in range(CB):
             nc.vector.scalar_tensor_tensor(
                 t_tm[:, block(b)], centred_gained[:, block(b)], rstd_x, shift_a_rows[:, block(b)], ALU.mult, ALU.add
             )
 
-        t_ps = psum_bank(C, "t_ps")
+        t_cm = held.tile([P, C], F32, name="t_cm")
         for b in range(CB):
-            nc.tensor.transpose(t_ps[:, block(b)], t_tm[:, block(b)], identity[:])
+            t_ps = psum_bank(P, "t_ps")
+            nc.tensor.transpose(t_ps[:], t_tm[:, block(b)], identity[:])
+            nc.scalar.activation(t_cm[:, block(b)], t_ps[:], ACT.Copy)
         keep_clock_up(WARM_AFTER_T, t_tm[:, block(CB - 1)])
 
         mean_t, rstd_t = mean_and_rstd([t_tm[:, block(b)] for b in range(CB)], "t")
@@ -123,6 +130,7 @@ def tile_crossdecoderlayer_kernel(
         normed_ps = [psum_bank(P, f"normed_ps{b}") for b in range(CB)]
         for b in range(CB):
             nc.tensor.transpose(normed_ps[b][:], normed_tm[:, block(b)], identity[:])
+        keep_clock_up(WARM_AFTER_NORMED, normed_tm[:, block(CB - 1)])
 
         y = held.tile([P, CB, N], BF16, name="y")
         for b in range(CB):
@@ -132,8 +140,6 @@ def tile_crossdecoderlayer_kernel(
                 nc.scalar.activation(y[:, b, :], normed_ps[b][:], ACT.Identity, bias=shift_col, scale=gain_col)
             else:
                 nc.vector.tensor_scalar(y[:, b, :], normed_ps[b][:], gain_col, shift_col, ALU.mult, ALU.add)
-        t_cm = held.tile([P, C], F32, name="t_cm")
-        nc.vector.tensor_copy(t_cm[:], t_ps[:])
 
         h = held.tile([P, FB, N], BF16, name="h")
         for kb in range(FB):

@@ -16,9 +16,6 @@ BN_STATS_DIM = 6
 PSUM_BANKS = 8
 FLOPS = 2 * 2 * C * F * N
 
-ROW_GAIN_B, ROW_SHIFT_B, ROW_B2, ROW_B1 = 0, CB, 2 * CB, 3 * CB
-N_ROWS = 32
-
 WARM_AFTER_X = 2
 WARM_AFTER_T = 3
 WARM_AFTER_NORMED = 1
@@ -57,63 +54,77 @@ def tile_crossdecoderlayer_kernel(
             for i in range(n_matmuls):
                 nc.tensor.matmul(unread[:, 0:P], identity[:], moving, start=True, stop=True)
 
-        x_cm = held.tile([P, CB, N], F32, name="x_cm")
-        x_blocks = x.rearrange("(b p) j -> p b j", p=P)
-        for half in range(2):
-            blocks = slice(half * CB // 2, (half + 1) * CB // 2)
-            nc.sync.dma_start(x_cm[:, blocks, :], x_blocks[:, blocks, :])
-        gain_a_rows = held.tile([P, C], F32, name="gain_a_rows")
-        nc.sync.dma_start(gain_a_rows[:], gain_a.rearrange("c o -> (c o)").partition_broadcast(P))
-        shift_a_rows = held.tile([P, C], F32, name="shift_a_rows")
-        nc.sync.dma_start(shift_a_rows[:], shift_a.rearrange("c o -> (c o)").partition_broadcast(P))
+        def load_columns(vec, name):
+            columns = held.tile([P, vec.shape[0] // P], F32, name=name)
+            nc.sync.dma_start(columns[:], vec.rearrange("(p i) o -> p (i o)", p=P))
+            return columns
 
-        vec_rows = held.tile([N_ROWS, P], F32, name="vec_rows")
-        nc.vector.memset(vec_rows[:], 0.0)
-        for row, vec in ((ROW_GAIN_B, gain_b), (ROW_SHIFT_B, shift_b), (ROW_B2, b2), (ROW_B1, b1)):
-            as_rows = vec.rearrange("(r p) o -> r (p o)", p=P)
-            nc.sync.dma_start(vec_rows[row : row + as_rows.shape[0], :], as_rows)
+        gain_a_cols = load_columns(gain_a, "gain_a_cols")
+        x_cm = held.tile([P, CB, N], F32, name="x_cm")
+        nc.sync.dma_start(x_cm[:], x.rearrange("(p b) j -> p b j", p=P))
+        shift_a_cols = load_columns(shift_a, "shift_a_cols")
+        gain_b_cols = load_columns(gain_b, "gain_b_cols")
+        shift_b_cols = load_columns(shift_b, "shift_b_cols")
+        b1_cols = load_columns(b1, "b1_cols")
+        b2_cols = load_columns(b2, "b2_cols")
+        w1_sb = held.tile([P, CB, F], BF16, name="w1_sb")
+        nc.sync.dma_start(w1_sb[:], w1.rearrange("(p b) k -> p b k", p=P))
+        w2_sb = held.tile([P, FB, C], BF16, name="w2_sb")
+        nc.sync.dma_start(w2_sb[:], w2.rearrange("(p kb) c -> p kb c", p=P))
         offsets = held.tile([P, N // 16], U16, name="offsets")
         nc.sync.dma_start(offsets[:], offs)
-        w1_sb = held.tile([P, CB, F], BF16, name="w1_sb")
-        nc.sync.dma_start(w1_sb[:], w1.rearrange("(b p) k -> p b k", p=P))
-        w2_sb = held.tile([P, FB, C], BF16, name="w2_sb")
-        nc.sync.dma_start(w2_sb[:], w2.rearrange("(kb p) c -> p kb c", p=P))
         windows = [held.tile([P, S], F32, name=f"window{b}") for b in range(CB)]
+        base_blocks = base.rearrange("(p b) s -> p b s", p=P)
+        out_blocks = out.rearrange("(p b) s -> p b s", p=P)
         for b in range(CB):
-            nc.sync.dma_start(windows[b][:], base[block(b), :])
+            nc.sync.dma_start(windows[b][:], base_blocks[:, b, :])
 
-        zeros = held.tile([P, BANK_F32], BF16, name="zeros")
+        zeros = held.tile([P, P], BF16, name="zeros")
         nc.vector.memset(zeros[:], 0.0)
         unread = psum_bank(BANK_F32, "unread")
         for i in range(WARM_BEFORE_X):
-            nc.tensor.matmul(unread[:], zeros[:, 0:P], zeros[:], start=True, stop=True)
+            nc.tensor.matmul(
+                unread[:].rearrange("p (r n) -> p r n", n=P),
+                zeros[:],
+                zeros[:].unsqueeze(1).to_broadcast([P, BANK_F32 // P, P]),
+                start=True,
+                stop=True,
+            )
 
         identity = held.tile([P, P], F32, name="identity")
         make_identity(nc, identity[:])
         eps_col = held.tile([P, 1], F32, name="eps_col")
         nc.gpsimd.memset(eps_col[:], EPS)
+        root_of_eps = held.tile([P, 1], F32, name="root_of_eps")
+        nc.scalar.activation(root_of_eps[:], eps_col[:], ACT.Abs_reciprocal_sqrt)
 
+        def spread_over_tokens(cols, name):
+            spread = psum_bank(C, name)
+            for b in range(CB):
+                nc.tensor.transpose(spread[:, block(b)], cols[:, b : b + 1].to_broadcast([P, P]), identity[:])
+            return spread
+
+        gain_a_ps = spread_over_tokens(gain_a_cols, "gain_a_ps")
+        gain_a_tm = held.tile([P, C], F32, name="gain_a_tm")
+        nc.scalar.activation(gain_a_tm[:], gain_a_ps[:], ACT.Copy)
         x_tm = [psum_bank(P, f"x_tm{b}") for b in range(CB)]
         for b in range(CB):
             nc.tensor.transpose(x_tm[b][:], x_cm[:, b, :], identity[:])
+        shift_a_tm = spread_over_tokens(shift_a_cols, "shift_a_tm")
         keep_clock_up(WARM_AFTER_X, x_cm[:, CB - 1, :])
-        vec_ps = psum_bank(N_ROWS, "vec_ps")
-        nc.tensor.matmul(vec_ps[:], vec_rows[:], identity[0:N_ROWS, 0:N_ROWS], start=True, stop=True)
 
         mean_x, rstd_x = mean_and_rstd([x_tm[b][:] for b in range(CB)], "x")
-        vec_cols = held.tile([P, N_ROWS], F32, name="vec_cols")
-        nc.scalar.activation(vec_cols[:], vec_ps[:], ACT.Copy)
         centred_gained = held.tile([P, C], F32, name="centred_gained")
         for b in range(CB):
             nc.vector.scalar_tensor_tensor(
-                centred_gained[:, block(b)], x_tm[b][:], mean_x, gain_a_rows[:, block(b)], ALU.subtract, ALU.mult
+                centred_gained[:, block(b)], x_tm[b][:], mean_x, gain_a_tm[:, block(b)], ALU.subtract, ALU.mult
             )
             if b % 2 == 0:
                 keep_clock_up(1, centred_gained[:, block(b)])
         t_tm = held.tile([P, C], F32, name="t_tm")
         for b in range(CB):
             nc.vector.scalar_tensor_tensor(
-                t_tm[:, block(b)], centred_gained[:, block(b)], rstd_x, shift_a_rows[:, block(b)], ALU.mult, ALU.add
+                t_tm[:, block(b)], centred_gained[:, block(b)], rstd_x, shift_a_tm[:, block(b)], ALU.mult, ALU.add
             )
 
         t_cm = held.tile([P, C], F32, name="t_cm")
@@ -134,8 +145,7 @@ def tile_crossdecoderlayer_kernel(
 
         y = held.tile([P, CB, N], BF16, name="y")
         for b in range(CB):
-            gain_col = vec_cols[:, ROW_GAIN_B + b : ROW_GAIN_B + b + 1]
-            shift_col = vec_cols[:, ROW_SHIFT_B + b : ROW_SHIFT_B + b + 1]
+            gain_col, shift_col = gain_b_cols[:, b : b + 1], shift_b_cols[:, b : b + 1]
             if b % 2 == 0:
                 nc.scalar.activation(y[:, b, :], normed_ps[b][:], ACT.Identity, bias=shift_col, scale=gain_col)
             else:
@@ -145,8 +155,8 @@ def tile_crossdecoderlayer_kernel(
         for kb in range(FB):
             h_ps = psum_bank(N, "h_ps")
             for b in range(CB):
-                nc.tensor.matmul(h_ps[:], w1_sb[:, b, block(kb)], y[:, b, :], start=(b == 0), stop=(b == CB - 1))
-            b1_col = vec_cols[:, ROW_B1 + kb : ROW_B1 + kb + 1]
+                nc.tensor.matmul(h_ps[:], w1_sb[:, b, kb::FB], y[:, b, :], start=(b == 0), stop=(b == CB - 1))
+            b1_col = b1_cols[:, kb : kb + 1]
             if kb % 2 == 0:
                 nc.scalar.activation(h[:, kb, :], h_ps[:], ACT.Relu, bias=b1_col)
             else:
@@ -155,8 +165,8 @@ def tile_crossdecoderlayer_kernel(
         for b in range(CB):
             u_ps = psum_bank(N, "u_ps")
             for kb in range(FB):
-                nc.tensor.matmul(u_ps[:], w2_sb[:, kb, block(b)], h[:, kb, :], start=(kb == 0), stop=(kb == FB - 1))
+                nc.tensor.matmul(u_ps[:], w2_sb[:, kb, b::CB], h[:, kb, :], start=(kb == 0), stop=(kb == FB - 1))
             u = ring.tile([P, N], F32, name="u")
-            nc.scalar.activation(u[:], u_ps[:], ACT.Identity, bias=vec_cols[:, ROW_B2 + b : ROW_B2 + b + 1])
+            nc.scalar.activation(u[:], u_ps[:], ACT.Identity, bias=b2_cols[:, b : b + 1])
             nc.vector.tensor_tensor(windows[b][:].indirect(offsets[:]), t_cm[:, block(b)], u[:], ALU.add)
-            nc.sync.dma_start(out[block(b), :], windows[b][:])
+            nc.sync.dma_start(out_blocks[:, b, :], windows[b][:])

@@ -59,16 +59,19 @@ def tile_crossdecoderlayer_kernel(
             nc.sync.dma_start(columns[:], vec.rearrange("(p i) o -> p (i o)", p=P))
             return columns
 
-        gain_a_cols = load_columns(gain_a, "gain_a_cols")
         x_cm = held.tile([P, CB, N], F32, name="x_cm")
-        nc.sync.dma_start(x_cm[:], x.rearrange("(p b) j -> p b j", p=P))
+        x_blocks = x.rearrange("(p b) j -> p b j", p=P)
+        for half in range(2):
+            blocks = slice(half * CB // 2, (half + 1) * CB // 2)
+            nc.sync.dma_start(x_cm[:, blocks, :], x_blocks[:, blocks, :])
+        gain_a_cols = load_columns(gain_a, "gain_a_cols")
         shift_a_cols = load_columns(shift_a, "shift_a_cols")
         gain_b_cols = load_columns(gain_b, "gain_b_cols")
         shift_b_cols = load_columns(shift_b, "shift_b_cols")
-        b1_cols = load_columns(b1, "b1_cols")
-        b2_cols = load_columns(b2, "b2_cols")
         w1_sb = held.tile([P, CB, F], BF16, name="w1_sb")
         nc.sync.dma_start(w1_sb[:], w1.rearrange("(p b) k -> p b k", p=P))
+        b1_cols = load_columns(b1, "b1_cols")
+        b2_cols = load_columns(b2, "b2_cols")
         w2_sb = held.tile([P, FB, C], BF16, name="w2_sb")
         nc.sync.dma_start(w2_sb[:], w2.rearrange("(p kb) c -> p kb c", p=P))
         offsets = held.tile([P, N // 16], U16, name="offsets")
@@ -98,19 +101,21 @@ def tile_crossdecoderlayer_kernel(
         root_of_eps = held.tile([P, 1], F32, name="root_of_eps")
         nc.scalar.activation(root_of_eps[:], eps_col[:], ACT.Abs_reciprocal_sqrt)
 
-        def spread_over_tokens(cols, name):
-            spread = psum_bank(C, name)
-            for b in range(CB):
-                nc.tensor.transpose(spread[:, block(b)], cols[:, b : b + 1].to_broadcast([P, P]), identity[:])
-            return spread
-
-        gain_a_ps = spread_over_tokens(gain_a_cols, "gain_a_ps")
-        gain_a_tm = held.tile([P, C], F32, name="gain_a_tm")
-        nc.scalar.activation(gain_a_tm[:], gain_a_ps[:], ACT.Copy)
         x_tm = [psum_bank(P, f"x_tm{b}") for b in range(CB)]
         for b in range(CB):
             nc.tensor.transpose(x_tm[b][:], x_cm[:, b, :], identity[:])
-        shift_a_tm = spread_over_tokens(shift_a_cols, "shift_a_tm")
+
+        def spread_over_tokens(cols, blocks, name):
+            spread = psum_bank(len(blocks) * P, name)
+            for i, b in enumerate(blocks):
+                nc.tensor.transpose(spread[:, block(i)], cols[:, b : b + 1].to_broadcast([P, P]), identity[:])
+            return spread
+
+        gain_a_tm = held.tile([P, C], F32, name="gain_a_tm")
+        for half in range(2):
+            gain_a_ps = spread_over_tokens(gain_a_cols, (2 * half, 2 * half + 1), f"gain_a_ps{half}")
+            nc.scalar.activation(gain_a_tm[:, half * C // 2 : (half + 1) * C // 2], gain_a_ps[:], ACT.Copy)
+        shift_a_tm = spread_over_tokens(shift_a_cols, range(CB), "shift_a_tm")
         keep_clock_up(WARM_AFTER_X, x_cm[:, CB - 1, :])
 
         mean_x, rstd_x = mean_and_rstd([x_tm[b][:] for b in range(CB)], "x")

@@ -51,8 +51,9 @@ def tile_crossdecoderlayer_kernel(
             return mean_var[:, 0:1], rstd[:]
 
         def keep_clock_up(n_matmuls, moving):
+            unread = psum_bank(P, "unread")
             for i in range(n_matmuls):
-                nc.tensor.matmul(unread[:, 0:P], identity[:], moving, start=True, stop=True)
+                nc.tensor.matmul(unread[:], identity[:], moving, start=True, stop=True)
 
         def load_columns(vec, name):
             columns = held.tile([P, vec.shape[0] // P], F32, name=name)
@@ -61,15 +62,14 @@ def tile_crossdecoderlayer_kernel(
 
         x_cm = held.tile([P, CB, N], F32, name="x_cm")
         x_blocks = x.rearrange("(p b) j -> p b j", p=P)
-        for half in range(2):
-            blocks = slice(half * CB // 2, (half + 1) * CB // 2)
-            nc.sync.dma_start(x_cm[:, blocks, :], x_blocks[:, blocks, :])
+        for b in range(CB):
+            nc.sync.dma_start(x_cm[:, b, :], x_blocks[:, b, :])
         gain_a_cols = load_columns(gain_a, "gain_a_cols")
         shift_a_cols = load_columns(shift_a, "shift_a_cols")
-        gain_b_cols = load_columns(gain_b, "gain_b_cols")
-        shift_b_cols = load_columns(shift_b, "shift_b_cols")
         w1_sb = held.tile([P, CB, F], BF16, name="w1_sb")
         nc.sync.dma_start(w1_sb[:], w1.rearrange("(p b) k -> p b k", p=P))
+        gain_b_cols = load_columns(gain_b, "gain_b_cols")
+        shift_b_cols = load_columns(shift_b, "shift_b_cols")
         b1_cols = load_columns(b1, "b1_cols")
         b2_cols = load_columns(b2, "b2_cols")
         w2_sb = held.tile([P, FB, C], BF16, name="w2_sb")
@@ -84,10 +84,10 @@ def tile_crossdecoderlayer_kernel(
 
         zeros = held.tile([P, P], BF16, name="zeros")
         nc.vector.memset(zeros[:], 0.0)
-        unread = psum_bank(BANK_F32, "unread")
+        unread_wide = psum_bank(BANK_F32, "unread_wide")
         for i in range(WARM_BEFORE_X):
             nc.tensor.matmul(
-                unread[:].rearrange("p (r n) -> p r n", n=P),
+                unread_wide[:].rearrange("p (r n) -> p r n", n=P),
                 zeros[:],
                 zeros[:].unsqueeze(1).to_broadcast([P, BANK_F32 // P, P]),
                 start=True,
@@ -105,17 +105,17 @@ def tile_crossdecoderlayer_kernel(
         for b in range(CB):
             nc.tensor.transpose(x_tm[b][:], x_cm[:, b, :], identity[:])
 
-        def spread_over_tokens(cols, blocks, name):
-            spread = psum_bank(len(blocks) * P, name)
-            for i, b in enumerate(blocks):
-                nc.tensor.transpose(spread[:, block(i)], cols[:, b : b + 1].to_broadcast([P, P]), identity[:])
-            return spread
+        def spread_over_tokens(spread, column):
+            nc.tensor.transpose(spread, column.to_broadcast([P, P]), identity[:])
 
         gain_a_tm = held.tile([P, C], F32, name="gain_a_tm")
-        for half in range(2):
-            gain_a_ps = spread_over_tokens(gain_a_cols, (2 * half, 2 * half + 1), f"gain_a_ps{half}")
-            nc.scalar.activation(gain_a_tm[:, half * C // 2 : (half + 1) * C // 2], gain_a_ps[:], ACT.Copy)
-        shift_a_tm = spread_over_tokens(shift_a_cols, range(CB), "shift_a_tm")
+        for b in range(CB):
+            gain_a_ps = psum_bank(P, "gain_a_ps")
+            spread_over_tokens(gain_a_ps[:], gain_a_cols[:, b : b + 1])
+            nc.scalar.activation(gain_a_tm[:, block(b)], gain_a_ps[:], ACT.Copy)
+        shift_a_tm = psum_bank(C, "shift_a_tm")
+        for b in range(CB):
+            spread_over_tokens(shift_a_tm[:, block(b)], shift_a_cols[:, b : b + 1])
         keep_clock_up(WARM_AFTER_X, x_cm[:, CB - 1, :])
 
         mean_x, rstd_x = mean_and_rstd([x_tm[b][:] for b in range(CB)], "x")

@@ -70,10 +70,11 @@ def tile_crossdecoderlayer_kernel(
         nc.sync.dma_start(w1_sb[:], w1.rearrange("(p b) k -> p b k", p=P))
         gain_b_cols = load_columns(gain_b, "gain_b_cols")
         shift_b_cols = load_columns(shift_b, "shift_b_cols")
-        b1_cols = load_columns(b1, "b1_cols")
+        b1_cols = held.tile([P, FB], F32, name="b1_cols")
+        nc.sync.dma_start(b1_cols[:], b1.rearrange("(kb p) o -> p (kb o)", p=P))
         b2_cols = load_columns(b2, "b2_cols")
         w2_sb = held.tile([P, FB, C], BF16, name="w2_sb")
-        nc.sync.dma_start(w2_sb[:], w2.rearrange("(p kb) c -> p kb c", p=P))
+        nc.sync.dma_start(w2_sb[:], w2.rearrange("(kb p) c -> p kb c", p=P))
         offsets = held.tile([P, N // 16], U16, name="offsets")
         nc.sync.dma_start(offsets[:], offs)
         windows = [held.tile([P, S], F32, name=f"window{b}") for b in range(CB)]
@@ -160,7 +161,7 @@ def tile_crossdecoderlayer_kernel(
         for kb in range(FB):
             h_ps = psum_bank(N, "h_ps")
             for b in range(CB):
-                nc.tensor.matmul(h_ps[:], w1_sb[:, b, kb::FB], y[:, b, :], start=(b == 0), stop=(b == CB - 1))
+                nc.tensor.matmul(h_ps[:], w1_sb[:, b, block(kb)], y[:, b, :], start=(b == 0), stop=(b == CB - 1))
             b1_col = b1_cols[:, kb : kb + 1]
             if kb % 2 == 0:
                 nc.scalar.activation(h[:, kb, :], h_ps[:], ACT.Relu, bias=b1_col)

import concourse.mybir as mybir
from concourse.masks import make_identity

F32 = mybir.dt.float32
BF16 = mybir.dt.bfloat16
U16 = mybir.dt.uint16
ALU = mybir.AluOpType
ACT = mybir.ActivationFunctionType

P = 128
C, F, S, N = 512, 1024, 512, 128
CB = C // P
FB = F // P
EPS = 1e-5
BN_STATS_DIM = 6
PSUM_BANKS = 8
FLOPS = 2 * 2 * C * F * N

WARM_AFTER_X = 2
WARM_AFTER_T = 3
WARM_AFTER_NORMED = 1
WARM_BEFORE_X = 3
BANK_F32 = 512


def block(i):
    return slice(i * P, (i + 1) * P)


def tile_crossdecoderlayer_kernel(
    tc, base, x, gain_a, shift_a, gain_b, shift_b, w1, b1, w2, b2, offs, out
):
    nc = tc.nc
    with (
        tc.tile_pool(name="held", bufs=1) as held,
        tc.tile_pool(name="ring", bufs=2) as ring,
        tc.psum_pool(name="psum", bufs=PSUM_BANKS) as psum,
    ):

        def psum_bank(width, name):
            return psum.tile([P, width], F32, name=name, tag="bank")

        def mean_and_rstd(blocks, name):
            stats = held.tile([P, CB * BN_STATS_DIM], F32, name=f"stats_{name}")
            for b in range(CB):
                nc.vector.bn_stats(stats[:, b * BN_STATS_DIM : (b + 1) * BN_STATS_DIM], blocks[b])
            mean_var = held.tile([P, 2], F32, name=f"mean_var_{name}")
            nc.vector.bn_aggr(mean_var[:], stats[:])
            rstd = held.tile([P, 1], F32, name=f"rstd_{name}")
            nc.scalar.activation(rstd[:], mean_var[:, 1:2], ACT.Abs_reciprocal_sqrt, bias=eps_col[:])
            return mean_var[:, 0:1], rstd[:]

        def keep_clock_up(n_matmuls, moving):
            unread = psum_bank(P, "unread")
            for i in range(n_matmuls):
                nc.tensor.matmul(unread[:], identity[:], moving, start=True, stop=True)

        def load_columns(vec, name):
            columns = held.tile([P, vec.shape[0] // P], F32, name=name)
            nc.sync.dma_start(columns[:], vec.rearrange("(p i) o -> p (i o)", p=P))
            return columns

        x_cm = held.tile([P, CB, N], F32, name="x_cm")
        x_blocks = x.rearrange("(p b) j -> p b j", p=P)
        for b in range(CB):
            nc.sync.dma_start(x_cm[:, b, :], x_blocks[:, b, :])
        gain_a_cols = load_columns(gain_a, "gain_a_cols")
        shift_a_cols = load_columns(shift_a, "shift_a_cols")
        w1_sb = held.tile([P, CB, F], BF16, name="w1_sb")
        nc.sync.dma_start(w1_sb[:], w1.rearrange("(p b) k -> p b k", p=P))
        gain_b_cols = load_columns(gain_b, "gain_b_cols")
        shift_b_cols = load_columns(shift_b, "shift_b_cols")
        b1_cols = held.tile([P, FB], F32, name="b1_cols")
        nc.sync.dma_start(b1_cols[:], b1.rearrange("(kb p) o -> p (kb o)", p=P))
        b2_cols = load_columns(b2, "b2_cols")
        w2_sb = held.tile([P, FB, C], BF16, name="w2_sb")
        nc.sync.dma_start(w2_sb[:], w2.rearrange("(kb p) c -> p kb c", p=P))
        offsets = held.tile([P, N // 16], U16, name="offsets")
        nc.sync.dma_start(offsets[:], offs)
        windows = [held.tile([P, S], F32, name=f"window{b}") for b in range(CB)]
        base_blocks = base.rearrange("(p b) s -> p b s", p=P)
        out_blocks = out.rearrange("(p b) s -> p b s", p=P)
        for b in range(CB):
            nc.sync.dma_start(windows[b][:], base_blocks[:, b, :])

        zeros = held.tile([P, P], BF16, name="zeros")
        nc.vector.memset(zeros[:], 0.0)
        unread_wide = psum_bank(BANK_F32, "unread_wide")
        for i in range(WARM_BEFORE_X):
            nc.tensor.matmul(
                unread_wide[:].rearrange("p (r n) -> p r n", n=P),
                zeros[:],
                zeros[:].unsqueeze(1).to_broadcast([P, BANK_F32 // P, P]),
                start=True,
                stop=True,
            )

        identity = held.tile([P, P], F32, name="identity")
        make_identity(nc, identity[:])
        eps_col = held.tile([P, 1], F32, name="eps_col")
        nc.gpsimd.memset(eps_col[:], EPS)
        root_of_eps = held.tile([P, 1], F32, name="root_of_eps")
        nc.scalar.activation(root_of_eps[:], eps_col[:], ACT.Abs_reciprocal_sqrt)

        x_tm = [psum_bank(P, f"x_tm{b}") for b in range(CB)]
        for b in range(CB):
            nc.tensor.transpose(x_tm[b][:], x_cm[:, b, :], identity[:])

        def spread_over_tokens(spread, column):
            nc.tensor.transpose(spread, column.to_broadcast([P, P]), identity[:])

        gain_a_tm = held.tile([P, C], F32, name="gain_a_tm")
        for b in range(CB):
            gain_a_ps = psum_bank(P, "gain_a_ps")
            spread_over_tokens(gain_a_ps[:], gain_a_cols[:, b : b + 1])
            nc.scalar.activation(gain_a_tm[:, block(b)], gain_a_ps[:], ACT.Copy)
        shift_a_tm = psum_bank(C, "shift_a_tm")
        for b in range(CB):
            spread_over_tokens(shift_a_tm[:, block(b)], shift_a_cols[:, b : b + 1])
        keep_clock_up(WARM_AFTER_X, x_cm[:, CB - 1, :])

        mean_x, rstd_x = mean_and_rstd([x_tm[b][:] for b in range(CB)], "x")
        centred_gained = held.tile([P, C], F32, name="centred_gained")
        for b in range(CB):
            nc.vector.scalar_tensor_tensor(
                centred_gained[:, block(b)], x_tm[b][:], mean_x, gain_a_tm[:, block(b)], ALU.subtract, ALU.mult
            )
            if b % 2 == 0:
                keep_clock_up(1, centred_gained[:, block(b)])
        t_tm = held.tile([P, C], F32, name="t_tm")
        for b in range(CB):
            nc.vector.scalar_tensor_tensor(
                t_tm[:, block(b)], centred_gained[:, block(b)], rstd_x, shift_a_tm[:, block(b)], ALU.mult, ALU.add
            )

        t_cm = held.tile([P, C], F32, name="t_cm")
        for b in range(CB):
            t_ps = psum_bank(P, "t_ps")
            nc.tensor.transpose(t_ps[:], t_tm[:, block(b)], identity[:])
            nc.scalar.activation(t_cm[:, block(b)], t_ps[:], ACT.Copy)
        keep_clock_up(WARM_AFTER_T, t_tm[:, block(CB - 1)])

        mean_t, rstd_t = mean_and_rstd([t_tm[:, block(b)] for b in range(CB)], "t")
        normed_tm = held.tile([P, C], F32, name="normed_tm")
        for b in range(CB):
            nc.vector.tensor_scalar(normed_tm[:, block(b)], t_tm[:, block(b)], mean_t, rstd_t, ALU.subtract, ALU.mult)
        normed_ps = [psum_bank(P, f"normed_ps{b}") for b in range(CB)]
        for b in range(CB):
            nc.tensor.transpose(normed_ps[b][:], normed_tm[:, block(b)], identity[:])
        keep_clock_up(WARM_AFTER_NORMED, normed_tm[:, block(CB - 1)])

        y = held.tile([P, CB, N], BF16, name="y")
        for b in range(CB):
            gain_col, shift_col = gain_b_cols[:, b : b + 1], shift_b_cols[:, b : b + 1]
            if b % 2 == 0:
                nc.scalar.activation(y[:, b, :], normed_ps[b][:], ACT.Identity, bias=shift_col, scale=gain_col)
            else:
                nc.vector.tensor_scalar(y[:, b, :], normed_ps[b][:], gain_col, shift_col, ALU.mult, ALU.add)

        h = held.tile([P, FB, N], BF16, name="h")
        for kb in range(FB):
            h_ps = psum_bank(N, "h_ps")
            for b in range(CB):
                nc.tensor.matmul(h_ps[:], w1_sb[:, b, block(kb)], y[:, b, :], start=(b == 0), stop=(b == CB - 1))
            b1_col = b1_cols[:, kb : kb + 1]
            if kb % 2 == 0:
                nc.scalar.activation(h[:, kb, :], h_ps[:], ACT.Relu, bias=b1_col)
            else:
                nc.vector.tensor_scalar(h[:, kb, :], h_ps[:], b1_col, 0.0, ALU.add, ALU.max)

        for b in range(CB):
            u_ps = psum_bank(N, "u_ps")
            for kb in range(FB):
                nc.tensor.matmul(u_ps[:], w2_sb[:, kb, b::CB], h[:, kb, :], start=(kb == 0), stop=(kb == FB - 1))
            u = ring.tile([P, N], F32, name="u")
            nc.scalar.activation(u[:], u_ps[:], ACT.Identity, bias=b2_cols[:, b : b + 1])
            nc.vector.tensor_tensor(windows[b][:].indirect(offsets[:]), t_cm[:, block(b)], u[:], ALU.add)
            nc.sync.dma_start(out_blocks[:, b, :], windows[b][:])
